import numpy as np
import ml_dtypes


def mxq(x, axis, fmt="e4m3"):
    dtype, down = {"e4m3": (ml_dtypes.float8_e4m3fn, 7), "e5m2": (ml_dtypes.float8_e5m2, 14)}[fmt]
    v = np.moveaxis(np.asarray(x, np.float32).astype(ml_dtypes.bfloat16).astype(np.float64), axis, -1)
    blocks = v.reshape(v.shape[:-1] + (-1, 32))
    amax = np.abs(blocks).max(-1, keepdims=True)
    byte = np.maximum(np.where(amax > 0, np.frexp(amax)[1] - 1 + 127, 0) - down, 1)
    scale = np.exp2(byte - 127.0)
    codes = (blocks / scale).astype(np.float32).astype(dtype).astype(np.float64)
    return np.moveaxis((codes * scale).reshape(v.shape), -1, axis)


WIDE = False


def mx_kscale(k):
    if not WIDE:
        return np.ones(k)
    levels = np.array([20, -20, 10, -10, 0])
    a = np.random.permutation(np.resize(levels, k // 512 * 4)).reshape(k // 512, 4)
    idx = np.arange(k)
    return np.exp2(a[idx // 512, idx % 128 // 32])


BF16 = ml_dtypes.bfloat16


def bf(x):
    return np.asarray(x, np.float32).astype(BF16)


def f64(x):
    return np.asarray(x).astype(np.float64)


C, G, P, E = 4096, 1024, 8, 64
J = P * E


def setup_inputs():
    u = mx_kscale(J)
    x = np.random.standard_normal((C, G))
    mask = np.random.randint(0, 2, (G, P))
    W = np.random.standard_normal((G, J)) * 1.4 / np.sqrt(G) / u[None, :]
    b = np.random.standard_normal(J) * 0.3
    g = np.random.standard_normal((C, P, E)) * np.exp2(np.random.randint(-12, 1, (C, 1, 1))) * 4.0
    g = np.ascontiguousarray(g * u.reshape(E, P).T[None, :, :])
    return {"x": bf(x), "mask": bf(mask), "W": bf(W), "b": bf(b), "grad_out": bf(g)}


def reference(x, mask, W, b, grad_out):
    wm = f64(W) * np.repeat(f64(mask), E, axis=1)
    gy = f64(grad_out).transpose(0, 2, 1).reshape(C, J)
    return mxq(gy, 1, "e5m2") @ mxq(wm, 1, "e4m3").T

@@ -1,0 +1,200 @@
+from contextlib import ExitStack
+
+import concourse.mybir as mybir
+from concourse.masks import make_identity
+
+F32 = mybir.dt.float32
+BF16 = mybir.dt.bfloat16
+U32 = mybir.dt.uint32
+U8 = mybir.dt.uint8
+E4M3X4 = mybir.dt.float8_e4m3fn_x4
+E5M2X4 = mybir.dt.float8_e5m2_x4
+
+P = 128
+C, G, J = 4096, 1024, 512
+NROW = C // P
+CH = 4
+NCH = NROW // CH
+FLOPS = 2 * C * G * J
+BYTES = C * J * 2 + G * J * 2 + G * 8 * 2 + C * G * 4
+
+LOAD_ROWS = [4, 4, 8, 8, 8]
+MANUAL = True
+
+
+def tile_featureembed_t_kernel(tc, x, mask, W, b, grad_out, out):
+    nc = tc.nc
+    gy_d = grad_out.rearrange("(q n) p e -> q (n p e)", n=NROW)
+    out_d = out.rearrange("(q n) g -> q (n g)", n=NROW)
+    w_d = W.rearrange("(t q) j -> q t j", q=P)
+    m_d = mask.rearrange("(t q) m -> q t m", q=P)
+
+    with ExitStack() as ctx:
+        keep = ctx.enter_context(tc.tile_pool(name="keep", bufs=1))
+        perm = ctx.enter_context(tc.tile_pool(name="perm", bufs=3))
+        grp = ctx.enter_context(tc.tile_pool(name="grp", bufs=3))
+        stage = ctx.enter_context(tc.tile_pool(name="stage", bufs=6))
+        psum = ctx.enter_context(tc.psum_pool(name="psum", bufs=8))
+        if MANUAL:
+            ctx.enter_context(tc.manual_schedule())
+
+        mask_sb = keep.tile([P, 8, 16], BF16, name="mask_sb")
+        nc.scalar.dma_start(out=mask_sb[:, :, 0:8], in_=m_d)
+        w_raw = []
+        for h in range(2):
+            t = keep.tile([P, 4 * J], BF16, name="w_raw%d" % h)
+            nc.sync.dma_start(
+                out=t[:].rearrange("q (t j) -> q t j", j=J), in_=w_d[:, 4 * h : 4 * h + 4, :]
+            )
+            w_raw.append(t)
+        raw_of_chunk = []
+        n0 = 0
+        for i, rows in enumerate(LOAD_ROWS):
+            t = keep.tile([P, rows * J], BF16, name="gy_raw%d" % i)
+            nc.sync.dma_start(out=t[:], in_=gy_d[:, n0 * J : (n0 + rows) * J])
+            for c in range(rows // CH):
+                raw_of_chunk.append((t, c * CH * J))
+            n0 += rows
+
+        ident = keep.tile([P, P], F32, name="ident")
+        make_identity(nc, ident[:])
+
+        mask32 = keep.tile([P, 256], BF16, name="mask32")
+        nc.vector.tensor_copy(
+            out=mask32[:].rearrange("q (t m r) -> q t m r", t=8, m=8),
+            in_=mask_sb[:, :, 0:8].unsqueeze(3).to_broadcast([P, 8, 8, 4]),
+        )
+        wm = [keep.tile([P, 4 * J], BF16, name="wm%d" % h) for h in range(2)]
+        wg = [keep.tile([P, 4 * J], BF16, name="wg%d" % h, align_bytes=64) for h in range(2)]
+        w_codes = [keep.tile([P, J], U32, name="w_codes%d" % h, align_bytes=64) for h in range(2)]
+        w_scales = [keep.tile([P, J], U8, name="w_scales%d" % h, align_bytes=64) for h in range(2)]
+
+        def w_mul(h, pc):
+            nc.vector.tensor_tensor(
+                out=wm[h][:, pc * 1024 : (pc + 1) * 1024].rearrange(
+                    "q (a b d) -> q a b d", b=4, d=2
+                ),
+                in0=w_raw[h][:].rearrange("q (a d c b) -> q c a b d", d=2, c=2, b=4)[:, pc],
+                in1=mask32[:, h * P : (h + 1) * P].unsqueeze(2).unsqueeze(3).to_broadcast([P, P, 4, 2]),
+                op=mybir.AluOpType.mult,
+            )
+
+        def w_bank(bk):
+            h = bk // 2
+            pw = psum.tile([P, 512], F32, name="pw", tag="bank")
+            pw4 = pw[:].rearrange("q (a u g) -> q a u g", a=2, u=2)
+            wm32 = wm[h][:].bitcast(F32)
+            for a in range(2):
+                gtl = (bk % 2) * 2 + a
+                for u in range(2):
+                    o = u * 512 + gtl * P
+                    nc.tensor.transpose(pw4[:, a, u, :], wm32[:, o : o + P], ident[:])
+            lo = (bk % 2) * 512
+            nc.scalar.copy(
+                out=wg[h][:].bitcast(F32)[:, lo : lo + 512].rearrange(
+                    "q (a g u) -> q a g u", a=2, u=2
+                ),
+                in_=pw[:].rearrange("q (a u g) -> q a g u", a=2, u=2),
+            )
+
+        def w_quant(h):
+            nc.vector.quantize_mx(
+                out=w_codes[h][:].bitcast(E4M3X4), scales=w_scales[h][:], in_=wg[h][:]
+            )
+
+        g_perm = {}
+        g_grp = {}
+        g_codes = {}
+        g_scales = {}
+
+        def pp(k):
+            t, off = raw_of_chunk[k]
+            gp = perm.tile([P, CH * J], BF16, name="gp")
+            nc.vector.tensor_copy(
+                out=gp[:].bitcast(F32).rearrange("q (x e a) -> q x e a", e=32, a=4),
+                in_=t[:, off : off + CH * J].bitcast(F32).rearrange(
+                    "q (x a e) -> q x e a", e=32, a=4
+                ),
+            )
+            g_perm[k] = gp
+
+        def tr(k):
+            gp32 = g_perm[k][:].bitcast(F32)
+            gg = grp.tile([P, CH * J], BF16, name="gg", align_bytes=64)
+            g_grp[k] = gg
+            for half in range(2):
+                pt = psum.tile([P, 512], F32, name="pt", tag="bank")
+                pt4 = pt[:].rearrange("q (a u c) -> q a u c", a=2, u=2)
+                for a in range(2):
+                    for u in range(2):
+                        o = ((half * 2 + a) * 2 + u) * P
+                        nc.tensor.transpose(pt4[:, a, u, :], gp32[:, o : o + P], ident[:])
+                nc.scalar.copy(
+                    out=gg[:].bitcast(F32)[:, half * 512 : (half + 1) * 512].rearrange(
+                        "q (a c u) -> q a c u", a=2, u=2
+                    ),
+                    in_=pt[:].rearrange("q (a u c) -> q a c u", a=2, u=2),
+                )
+
+        def qz(k):
+            cd = keep.tile([P, CH * P], U32, name="g_codes%d" % k, align_bytes=64)
+            sc = keep.tile([P, CH * P], U8, name="g_scales%d" % k, align_bytes=64)
+            nc.vector.quantize_mx(out=cd[:].bitcast(E5M2X4), scales=sc[:], in_=g_grp[k][:])
+            g_codes[k] = cd
+            g_scales[k] = sc
+
+        st_of_pair = {}
+
+        def mx(k, nn):
+            n = k * CH + nn
+            if n % 2 == 0:
+                st_of_pair[n // 2] = stage.tile([P, 2 * G], F32, name="st")
+            st = st_of_pair[n // 2]
+            for h in range(2):
+                po = psum.tile([P, 512], F32, name="po", tag="bank")
+                nc.tensor.matmul_mx(
+                    out=po[:],
+                    lhsT=g_codes[k][:, nn * P : (nn + 1) * P].bitcast(E5M2X4),
+                    lhsT_scale=g_scales[k][:, nn * P : (nn + 1) * P],
+                    rhs=w_codes[h][:].bitcast(E4M3X4),
+                    rhs_scale=w_scales[h][:],
+                    start=True,
+                    stop=True,
+                )
+                lo = (n % 2) * G + h * 512
+                if h == 0:
+                    nc.scalar.copy(out=st[:, lo : lo + 512], in_=po[:])
+                else:
+                    nc.vector.tensor_copy(out=st[:, lo : lo + 512], in_=po[:])
+            if n < 2:
+                lo = (n % 2) * G
+                nc.sync.dma_start(out=out_d[:, n * G : (n + 1) * G], in_=st[:, lo : lo + G])
+            elif n % 2 == 1:
+                nc.sync.dma_start(out=out_d[:, (n - 1) * G : (n + 1) * G], in_=st[:])
+
+        w_mul(0, 0)
+        w_mul(0, 1)
+        w_bank(0)
+        w_bank(1)
+        pp(0)
+        tr(0)
+        w_mul(1, 0)
+        w_mul(1, 1)
+        w_bank(2)
+        w_bank(3)
+        pp(1)
+        tr(1)
+        w_quant(0)
+        qz(0)
+        w_quant(1)
+        for k in range(NCH):
+            if k + 1 < NCH:
+                qz(k + 1)
+            mx(k, 0)
+            mx(k, 1)
+            if k + 2 < NCH:
+                pp(k + 2)
+            mx(k, 2)
+            mx(k, 3)
+            if k + 2 < NCH:
+                tr(k + 2)

@@ -18,7 +18,8 @@ NCH = NROW // CH
 FLOPS = 2 * C * G * J
 BYTES = C * J * 2 + G * J * 2 + G * 8 * 2 + C * G * 4
 
-LOAD_ROWS = [4, 4, 8, 8, 8]
+LOADS = [("w", 0), ("w", 1), ("g", 4), ("w", 2), ("w", 3), ("g", 4), ("g", 8), ("g", 8), ("g", 8)]
+SINGLE = 8
 MANUAL = True
 
 
@@ -34,6 +35,7 @@ def tile_featureembed_t_kernel(tc, x, mask, W, b, grad_out, out):
         perm = ctx.enter_context(tc.tile_pool(name="perm", bufs=3))
         grp = ctx.enter_context(tc.tile_pool(name="grp", bufs=3))
         stage = ctx.enter_context(tc.tile_pool(name="stage", bufs=6))
+        stage1 = ctx.enter_context(tc.tile_pool(name="stage1", bufs=4))
         psum = ctx.enter_context(tc.psum_pool(name="psum", bufs=8))
         if MANUAL:
             ctx.enter_context(tc.manual_schedule())
@@ -41,20 +43,21 @@ def tile_featureembed_t_kernel(tc, x, mask, W, b, grad_out, out):
         mask_sb = keep.tile([P, 8, 16], BF16, name="mask_sb")
         nc.scalar.dma_start(out=mask_sb[:, :, 0:8], in_=m_d)
         w_raw = []
-        for h in range(2):
-            t = keep.tile([P, 4 * J], BF16, name="w_raw%d" % h)
-            nc.sync.dma_start(
-                out=t[:].rearrange("q (t j) -> q t j", j=J), in_=w_d[:, 4 * h : 4 * h + 4, :]
-            )
-            w_raw.append(t)
         raw_of_chunk = []
         n0 = 0
-        for i, rows in enumerate(LOAD_ROWS):
-            t = keep.tile([P, rows * J], BF16, name="gy_raw%d" % i)
-            nc.sync.dma_start(out=t[:], in_=gy_d[:, n0 * J : (n0 + rows) * J])
-            for c in range(rows // CH):
-                raw_of_chunk.append((t, c * CH * J))
-            n0 += rows
+        for kind, v in LOADS:
+            if kind == "w":
+                t = keep.tile([P, 2 * J], BF16, name="w_raw%d" % v)
+                nc.sync.dma_start(
+                    out=t[:].rearrange("q (t j) -> q t j", j=J), in_=w_d[:, 2 * v : 2 * v + 2, :]
+                )
+                w_raw.append(t)
+            else:
+                t = keep.tile([P, v * J], BF16, name="gy_raw%d" % n0)
+                nc.sync.dma_start(out=t[:], in_=gy_d[:, n0 * J : (n0 + v) * J])
+                for c in range(v // CH):
+                    raw_of_chunk.append((t, c * CH * J))
+                n0 += v
 
         ident = keep.tile([P, P], F32, name="ident")
         make_identity(nc, ident[:])
@@ -64,18 +67,18 @@ def tile_featureembed_t_kernel(tc, x, mask, W, b, grad_out, out):
             out=mask32[:].rearrange("q (t m r) -> q t m r", t=8, m=8),
             in_=mask_sb[:, :, 0:8].unsqueeze(3).to_broadcast([P, 8, 8, 4]),
         )
-        wm = [keep.tile([P, 4 * J], BF16, name="wm%d" % h) for h in range(2)]
+        wm = [keep.tile([P, 2 * J], BF16, name="wm%d" % bk) for bk in range(4)]
         wg = [keep.tile([P, 4 * J], BF16, name="wg%d" % h, align_bytes=64) for h in range(2)]
         w_codes = [keep.tile([P, J], U32, name="w_codes%d" % h, align_bytes=64) for h in range(2)]
         w_scales = [keep.tile([P, J], U8, name="w_scales%d" % h, align_bytes=64) for h in range(2)]
 
-        def w_mul(h, pc):
+        def w_mul(bk, pc):
             nc.vector.tensor_tensor(
-                out=wm[h][:, pc * 1024 : (pc + 1) * 1024].rearrange(
+                out=wm[bk][:, pc * 512 : (pc + 1) * 512].rearrange(
                     "q (a b d) -> q a b d", b=4, d=2
                 ),
-                in0=w_raw[h][:].rearrange("q (a d c b) -> q c a b d", d=2, c=2, b=4)[:, pc],
-                in1=mask32[:, h * P : (h + 1) * P].unsqueeze(2).unsqueeze(3).to_broadcast([P, P, 4, 2]),
+                in0=w_raw[bk][:].rearrange("q (a d c b) -> q c a b d", d=2, c=2, b=4)[:, pc],
+                in1=mask32[:, bk * 64 : (bk + 1) * 64].unsqueeze(2).unsqueeze(3).to_broadcast([P, 64, 4, 2]),
                 op=mybir.AluOpType.mult,
             )
 
@@ -83,11 +86,10 @@ def tile_featureembed_t_kernel(tc, x, mask, W, b, grad_out, out):
             h = bk // 2
             pw = psum.tile([P, 512], F32, name="pw", tag="bank")
             pw4 = pw[:].rearrange("q (a u g) -> q a u g", a=2, u=2)
-            wm32 = wm[h][:].bitcast(F32)
+            wm32 = wm[bk][:].bitcast(F32)
             for a in range(2):
-                gtl = (bk % 2) * 2 + a
                 for u in range(2):
-                    o = u * 512 + gtl * P
+                    o = u * 256 + a * P
                     nc.tensor.transpose(pw4[:, a, u, :], wm32[:, o : o + P], ident[:])
             lo = (bk % 2) * 512
             nc.scalar.copy(
@@ -107,15 +109,15 @@ def tile_featureembed_t_kernel(tc, x, mask, W, b, grad_out, out):
         g_codes = {}
         g_scales = {}
 
-        def pp(k):
+        def pp(k, on_scalar=False):
             t, off = raw_of_chunk[k]
             gp = perm.tile([P, CH * J], BF16, name="gp")
-            nc.vector.tensor_copy(
-                out=gp[:].bitcast(F32).rearrange("q (x e a) -> q x e a", e=32, a=4),
-                in_=t[:, off : off + CH * J].bitcast(F32).rearrange(
-                    "q (x a e) -> q x e a", e=32, a=4
-                ),
-            )
+            dst = gp[:].bitcast(F32).rearrange("q (x e a) -> q x e a", e=32, a=4)
+            src = t[:, off : off + CH * J].bitcast(F32).rearrange("q (x a e) -> q x e a", e=32, a=4)
+            if on_scalar:
+                nc.scalar.copy(out=dst, in_=src)
+            else:
+                nc.vector.tensor_copy(out=dst, in_=src)
             g_perm[k] = gp
 
         def tr(k):
@@ -147,9 +149,12 @@ def tile_featureembed_t_kernel(tc, x, mask, W, b, grad_out, out):
 
         def mx(k, nn):
             n = k * CH + nn
-            if n % 2 == 0:
-                st_of_pair[n // 2] = stage.tile([P, 2 * G], F32, name="st")
-            st = st_of_pair[n // 2]
+            if n < SINGLE:
+                st = stage1.tile([P, G], F32, name="st1")
+            else:
+                if n % 2 == 0:
+                    st_of_pair[n // 2] = stage.tile([P, 2 * G], F32, name="st")
+                st = st_of_pair[n // 2]
             for h in range(2):
                 po = psum.tile([P, 512], F32, name="po", tag="bank")
                 nc.tensor.matmul_mx(
@@ -161,40 +166,51 @@ def tile_featureembed_t_kernel(tc, x, mask, W, b, grad_out, out):
                     start=True,
                     stop=True,
                 )
-                lo = (n % 2) * G + h * 512
+                lo = h * 512 if n < SINGLE else (n % 2) * G + h * 512
                 if h == 0:
                     nc.scalar.copy(out=st[:, lo : lo + 512], in_=po[:])
                 else:
                     nc.vector.tensor_copy(out=st[:, lo : lo + 512], in_=po[:])
-            if n < 2:
-                lo = (n % 2) * G
-                nc.sync.dma_start(out=out_d[:, n * G : (n + 1) * G], in_=st[:, lo : lo + G])
+            if n < SINGLE:
+                nc.sync.dma_start(out=out_d[:, n * G : (n + 1) * G], in_=st[:])
             elif n % 2 == 1:
                 nc.sync.dma_start(out=out_d[:, (n - 1) * G : (n + 1) * G], in_=st[:])
 
+        pp(0, on_scalar=True)
         w_mul(0, 0)
         w_mul(0, 1)
         w_bank(0)
-        w_bank(1)
-        pp(0)
-        tr(0)
         w_mul(1, 0)
         w_mul(1, 1)
+        w_bank(1)
+        tr(0)
+        w_mul(2, 0)
+        w_mul(2, 1)
         w_bank(2)
+        w_mul(3, 0)
+        w_mul(3, 1)
         w_bank(3)
         pp(1)
-        tr(1)
         w_quant(0)
         qz(0)
         w_quant(1)
-        for k in range(NCH):
+        tr(1)
+        mx(0, 0)
+        mx(0, 1)
+        qz(1)
+        pp(2)
+        mx(0, 2)
+        mx(0, 3)
+        tr(2)
+        pp(3)
+        for k in range(1, NCH):
+            mx(k, 0)
             if k + 1 < NCH:
                 qz(k + 1)
-            mx(k, 0)
             mx(k, 1)
             if k + 2 < NCH:
-                pp(k + 2)
-            mx(k, 2)
-            mx(k, 3)
-            if k + 2 < NCH:
                 tr(k + 2)
+            mx(k, 2)
+            if k + 3 < NCH:
+                pp(k + 3)
+            mx(k, 3)

@@ -19,7 +19,8 @@ FLOPS = 2 * C * G * J
 BYTES = C * J * 2 + G * J * 2 + G * 8 * 2 + C * G * 4
 
 LOADS = [("w", 0), ("w", 1), ("g", 4), ("w", 2), ("w", 3), ("g", 4), ("g", 8), ("g", 8), ("g", 8)]
-SINGLE = 8
+STORE_ROWS = [1] * 8 + [2] * 6 + [4] * 3
+STAGE_BUFS = {1: 6, 2: 4, 4: 3}
 MANUAL = True
 
 
@@ -34,8 +35,10 @@ def tile_featureembed_t_kernel(tc, x, mask, W, b, grad_out, out):
         keep = ctx.enter_context(tc.tile_pool(name="keep", bufs=1))
         perm = ctx.enter_context(tc.tile_pool(name="perm", bufs=3))
         grp = ctx.enter_context(tc.tile_pool(name="grp", bufs=3))
-        stage = ctx.enter_context(tc.tile_pool(name="stage", bufs=6))
-        stage1 = ctx.enter_context(tc.tile_pool(name="stage1", bufs=4))
+        stage = {
+            s: ctx.enter_context(tc.tile_pool(name="stage%d" % s, bufs=STAGE_BUFS[s]))
+            for s in STAGE_BUFS
+        }
         psum = ctx.enter_context(tc.psum_pool(name="psum", bufs=8))
         if MANUAL:
             ctx.enter_context(tc.manual_schedule())
@@ -145,16 +148,19 @@ def tile_featureembed_t_kernel(tc, x, mask, W, b, grad_out, out):
             g_codes[k] = cd
             g_scales[k] = sc
 
-        st_of_pair = {}
+        group_of_row = []
+        for s in STORE_ROWS:
+            first = len(group_of_row)
+            for i in range(s):
+                group_of_row.append((first, s))
+        st_of_group = {}
 
         def mx(k, nn):
             n = k * CH + nn
-            if n < SINGLE:
-                st = stage1.tile([P, G], F32, name="st1")
-            else:
-                if n % 2 == 0:
-                    st_of_pair[n // 2] = stage.tile([P, 2 * G], F32, name="st")
-                st = st_of_pair[n // 2]
+            first, s = group_of_row[n]
+            if n == first:
+                st_of_group[first] = stage[s].tile([P, s * G], F32, name="st%d" % s)
+            st = st_of_group[first]
             for h in range(2):
                 po = psum.tile([P, 512], F32, name="po", tag="bank")
                 nc.tensor.matmul_mx(
@@ -166,15 +172,13 @@ def tile_featureembed_t_kernel(tc, x, mask, W, b, grad_out, out):
                     start=True,
                     stop=True,
                 )
-                lo = h * 512 if n < SINGLE else (n % 2) * G + h * 512
+                lo = (n - first) * G + h * 512
                 if h == 0:
                     nc.scalar.copy(out=st[:, lo : lo + 512], in_=po[:])
                 else:
                     nc.vector.tensor_copy(out=st[:, lo : lo + 512], in_=po[:])
-            if n < SINGLE:
-                nc.sync.dma_start(out=out_d[:, n * G : (n + 1) * G], in_=st[:])
-            elif n % 2 == 1:
-                nc.sync.dma_start(out=out_d[:, (n - 1) * G : (n + 1) * G], in_=st[:])
+            if n == first + s - 1:
+                nc.sync.dma_start(out=out_d[:, first * G : (first + s) * G], in_=st[:])
 
         pp(0, on_scalar=True)
         w_mul(0, 0)
@@ -194,15 +198,15 @@ def tile_featureembed_t_kernel(tc, x, mask, W, b, grad_out, out):
         w_quant(0)
         qz(0)
         w_quant(1)
+        pp(2)
         tr(1)
         mx(0, 0)
         mx(0, 1)
         qz(1)
-        pp(2)
         mx(0, 2)
-        mx(0, 3)
         tr(2)
         pp(3)
+        mx(0, 3)
         for k in range(1, NCH):
             mx(k, 0)
             if k + 1 < NCH:

@@ -28,8 +28,8 @@ def tile_featureembed_t_kernel(tc, x, mask, W, b, grad_out, out):
     nc = tc.nc
     gy_d = grad_out.rearrange("(q n) p e -> q (n p e)", n=NROW)
     out_d = out.rearrange("(q n) g -> q (n g)", n=NROW)
-    w_d = W.rearrange("(t q) j -> q t j", q=P)
-    m_d = mask.rearrange("(t q) m -> q t m", q=P)
+    w_d = W.rearrange("(q t) j -> q t j", t=8)
+    m_d = mask.rearrange("(q t) m -> q (t m)", t=8)
 
     with ExitStack() as ctx:
         keep = ctx.enter_context(tc.tile_pool(name="keep", bufs=1))
@@ -43,8 +43,8 @@ def tile_featureembed_t_kernel(tc, x, mask, W, b, grad_out, out):
         if MANUAL:
             ctx.enter_context(tc.manual_schedule())
 
-        mask_sb = keep.tile([P, 8, 16], BF16, name="mask_sb")
-        nc.scalar.dma_start(out=mask_sb[:, :, 0:8], in_=m_d)
+        mask_sb = keep.tile([P, 64], BF16, name="mask_sb")
+        nc.sync.dma_start(out=mask_sb[:], in_=m_d)
         w_raw = []
         raw_of_chunk = []
         n0 = 0
@@ -67,8 +67,8 @@ def tile_featureembed_t_kernel(tc, x, mask, W, b, grad_out, out):
 
         mask32 = keep.tile([P, 256], BF16, name="mask32")
         nc.vector.tensor_copy(
-            out=mask32[:].rearrange("q (t m r) -> q t m r", t=8, m=8),
-            in_=mask_sb[:, :, 0:8].unsqueeze(3).to_broadcast([P, 8, 8, 4]),
+            out=mask32[:].rearrange("q (a r) -> q a r", r=4),
+            in_=mask_sb[:].unsqueeze(2).to_broadcast([P, 64, 4]),
         )
         wm = [keep.tile([P, 2 * J], BF16, name="wm%d" % bk) for bk in range(4)]
         wg = [keep.tile([P, 4 * J], BF16, name="wg%d" % h, align_bytes=64) for h in range(2)]
@@ -155,30 +155,39 @@ def tile_featureembed_t_kernel(tc, x, mask, W, b, grad_out, out):
                 group_of_row.append((first, s))
         st_of_group = {}
 
-        def mx(k, nn):
-            n = k * CH + nn
-            first, s = group_of_row[n]
-            if n == first:
-                st_of_group[first] = stage[s].tile([P, s * G], F32, name="st%d" % s)
-            st = st_of_group[first]
+        def pair(n):
+            k = n // CH
+            banks = {}
             for h in range(2):
-                po = psum.tile([P, 512], F32, name="po", tag="bank")
-                nc.tensor.matmul_mx(
-                    out=po[:],
-                    lhsT=g_codes[k][:, nn * P : (nn + 1) * P].bitcast(E5M2X4),
-                    lhsT_scale=g_scales[k][:, nn * P : (nn + 1) * P],
-                    rhs=w_codes[h][:].bitcast(E4M3X4),
-                    rhs_scale=w_scales[h][:],
-                    start=True,
-                    stop=True,
-                )
-                lo = (n - first) * G + h * 512
-                if h == 0:
-                    nc.scalar.copy(out=st[:, lo : lo + 512], in_=po[:])
-                else:
-                    nc.vector.tensor_copy(out=st[:, lo : lo + 512], in_=po[:])
-            if n == first + s - 1:
-                nc.sync.dma_start(out=out_d[:, first * G : (first + s) * G], in_=st[:])
+                for r in range(2):
+                    nn = n + r - k * CH
+                    po = psum.tile([P, 512], F32, name="po", tag="bank")
+                    nc.tensor.matmul_mx(
+                        out=po[:],
+                        lhsT=g_codes[k][:, nn * P : (nn + 1) * P].bitcast(E5M2X4),
+                        lhsT_scale=g_scales[k][:, nn * P : (nn + 1) * P],
+                        rhs=w_codes[h][:].bitcast(E4M3X4),
+                        rhs_scale=w_scales[h][:],
+                        start=True,
+                        stop=True,
+                    )
+                    banks[(r, h)] = po
+            for r in range(2):
+                row = n + r
+                first, s = group_of_row[row]
+                if row == first:
+                    st_of_group[first] = stage[s].tile([P, s * G], F32, name="st%d" % s)
+                st = st_of_group[first]
+                lo = (row - first) * G
+                dst = st[:, lo : lo + G].rearrange("c (q h t) -> c h q t", h=2, t=4)
+                for h in range(2):
+                    src = banks[(r, h)][:].rearrange("c (t q) -> c q t", t=4)
+                    if r == 0:
+                        nc.scalar.copy(out=dst[:, h], in_=src)
+                    else:
+                        nc.vector.tensor_copy(out=dst[:, h], in_=src)
+                if row == first + s - 1:
+                    nc.sync.dma_start(out=out_d[:, first * G : (first + s) * G], in_=st[:])
 
         pp(0, on_scalar=True)
         w_mul(0, 0)
@@ -200,21 +209,12 @@ def tile_featureembed_t_kernel(tc, x, mask, W, b, grad_out, out):
         w_quant(1)
         pp(2)
         tr(1)
-        mx(0, 0)
-        mx(0, 1)
-        qz(1)
-        mx(0, 2)
-        tr(2)
-        pp(3)
-        mx(0, 3)
-        for k in range(1, NCH):
-            mx(k, 0)
+        for k in range(NCH):
+            pair(k * CH)
             if k + 1 < NCH:
                 qz(k + 1)
-            mx(k, 1)
             if k + 2 < NCH:
                 tr(k + 2)
-            mx(k, 2)
             if k + 3 < NCH:
                 pp(k + 3)
-            mx(k, 3)
+            pair(k * CH + 2)

@@ -19,8 +19,8 @@ FLOPS = 2 * C * G * J
 BYTES = C * J * 2 + G * J * 2 + G * 8 * 2 + C * G * 4
 
 LOADS = [("w", 0), ("w", 1), ("g", 4), ("w", 2), ("w", 3), ("g", 4), ("g", 8), ("g", 8), ("g", 8)]
-STORE_ROWS = [1] * 8 + [2] * 6 + [4] * 3
-STAGE_BUFS = {1: 6, 2: 4, 4: 3}
+STORE_ROWS = [1] * 4 + [2] * 6 + [4] * 4
+STAGE_BUFS = {1: 4, 2: 5, 4: 3}
 MANUAL = True
 
 

@@ -65,6 +65,14 @@ def tile_featureembed_t_kernel(tc, x, mask, W, b, grad_out, out):
         ident = keep.tile([P, P], F32, name="ident")
         make_identity(nc, ident[:])
 
+        warm = keep.tile([P, 512], BF16, name="warm")
+        nc.vector.memset(warm[:], 0.0)
+
+        def dummy(n):
+            pd = psum.tile([P, 512], F32, name="pd", tag="bank")
+            for i in range(n):
+                nc.tensor.matmul(pd[:], lhsT=warm[:, 0:P], rhs=warm[:], start=True, stop=True)
+
         mask32 = keep.tile([P, 256], BF16, name="mask32")
         nc.vector.tensor_copy(
             out=mask32[:].rearrange("q (a r) -> q a r", r=4),
@@ -189,20 +197,26 @@ def tile_featureembed_t_kernel(tc, x, mask, W, b, grad_out, out):
                 if row == first + s - 1:
                     nc.sync.dma_start(out=out_d[:, first * G : (first + s) * G], in_=st[:])
 
+        dummy(6)
         pp(0, on_scalar=True)
         w_mul(0, 0)
         w_mul(0, 1)
         w_bank(0)
+        dummy(2)
         w_mul(1, 0)
         w_mul(1, 1)
         w_bank(1)
+        dummy(1)
         tr(0)
+        dummy(2)
         w_mul(2, 0)
         w_mul(2, 1)
         w_bank(2)
+        dummy(2)
         w_mul(3, 0)
         w_mul(3, 1)
         w_bank(3)
+        dummy(2)
         pp(1)
         w_quant(0)
         qz(0)

@@ -67,6 +67,8 @@ def tile_featureembed_t_kernel(tc, x, mask, W, b, grad_out, out):
 
         warm = keep.tile([P, 512], BF16, name="warm")
         nc.vector.memset(warm[:], 0.0)
+        act_first = keep.tile([P, 2], BF16, name="act_first")
+        nc.scalar.copy(out=act_first[:, 0:1], in_=warm[:, 0:1])
 
         def dummy(n):
             pd = psum.tile([P, 512], F32, name="pd", tag="bank")

from contextlib import ExitStack

import concourse.mybir as mybir
from concourse.masks import make_identity

F32 = mybir.dt.float32
BF16 = mybir.dt.bfloat16
U32 = mybir.dt.uint32
U8 = mybir.dt.uint8
E4M3X4 = mybir.dt.float8_e4m3fn_x4
E5M2X4 = mybir.dt.float8_e5m2_x4

P = 128
C, G, J = 4096, 1024, 512
NROW = C // P
CH = 4
NCH = NROW // CH
FLOPS = 2 * C * G * J
BYTES = C * J * 2 + G * J * 2 + G * 8 * 2 + C * G * 4

LOADS = [("w", 0), ("w", 1), ("g", 4), ("w", 2), ("w", 3), ("g", 4), ("g", 8), ("g", 8), ("g", 8)]
STORE_ROWS = [1] * 4 + [2] * 6 + [4] * 4
STAGE_BUFS = {1: 4, 2: 5, 4: 3}
MANUAL = True


def tile_featureembed_t_kernel(tc, x, mask, W, b, grad_out, out):
    nc = tc.nc
    gy_d = grad_out.rearrange("(q n) p e -> q (n p e)", n=NROW)
    out_d = out.rearrange("(q n) g -> q (n g)", n=NROW)
    w_d = W.rearrange("(q t) j -> q t j", t=8)
    m_d = mask.rearrange("(q t) m -> q (t m)", t=8)

    with ExitStack() as ctx:
        keep = ctx.enter_context(tc.tile_pool(name="keep", bufs=1))
        perm = ctx.enter_context(tc.tile_pool(name="perm", bufs=3))
        grp = ctx.enter_context(tc.tile_pool(name="grp", bufs=3))
        stage = {
            s: ctx.enter_context(tc.tile_pool(name="stage%d" % s, bufs=STAGE_BUFS[s]))
            for s in STAGE_BUFS
        }
        psum = ctx.enter_context(tc.psum_pool(name="psum", bufs=8))
        if MANUAL:
            ctx.enter_context(tc.manual_schedule())

        mask_sb = keep.tile([P, 64], BF16, name="mask_sb")
        nc.sync.dma_start(out=mask_sb[:], in_=m_d)
        w_raw = []
        raw_of_chunk = []
        n0 = 0
        for kind, v in LOADS:
            if kind == "w":
                t = keep.tile([P, 2 * J], BF16, name="w_raw%d" % v)
                nc.sync.dma_start(
                    out=t[:].rearrange("q (t j) -> q t j", j=J), in_=w_d[:, 2 * v : 2 * v + 2, :]
                )
                w_raw.append(t)
            else:
                t = keep.tile([P, v * J], BF16, name="gy_raw%d" % n0)
                nc.sync.dma_start(out=t[:], in_=gy_d[:, n0 * J : (n0 + v) * J])
                for c in range(v // CH):
                    raw_of_chunk.append((t, c * CH * J))
                n0 += v

        ident = keep.tile([P, P], F32, name="ident")
        make_identity(nc, ident[:])

        warm = keep.tile([P, 512], BF16, name="warm")
        nc.vector.memset(warm[:], 0.0)
        act_first = keep.tile([P, 2], BF16, name="act_first")
        nc.scalar.copy(out=act_first[:, 0:1], in_=warm[:, 0:1])

        def dummy(n):
            pd = psum.tile([P, 512], F32, name="pd", tag="bank")
            for i in range(n):
                nc.tensor.matmul(pd[:], lhsT=warm[:, 0:P], rhs=warm[:], start=True, stop=True)

        mask32 = keep.tile([P, 256], BF16, name="mask32")
        nc.vector.tensor_copy(
            out=mask32[:].rearrange("q (a r) -> q a r", r=4),
            in_=mask_sb[:].unsqueeze(2).to_broadcast([P, 64, 4]),
        )
        wm = [keep.tile([P, 2 * J], BF16, name="wm%d" % bk) for bk in range(4)]
        wg = [keep.tile([P, 4 * J], BF16, name="wg%d" % h, align_bytes=64) for h in range(2)]
        w_codes = [keep.tile([P, J], U32, name="w_codes%d" % h, align_bytes=64) for h in range(2)]
        w_scales = [keep.tile([P, J], U8, name="w_scales%d" % h, align_bytes=64) for h in range(2)]

        def w_mul(bk, pc):
            nc.vector.tensor_tensor(
                out=wm[bk][:, pc * 512 : (pc + 1) * 512].rearrange(
                    "q (a b d) -> q a b d", b=4, d=2
                ),
                in0=w_raw[bk][:].rearrange("q (a d c b) -> q c a b d", d=2, c=2, b=4)[:, pc],
                in1=mask32[:, bk * 64 : (bk + 1) * 64].unsqueeze(2).unsqueeze(3).to_broadcast([P, 64, 4, 2]),
                op=mybir.AluOpType.mult,
            )

        def w_bank(bk):
            h = bk // 2
            pw = psum.tile([P, 512], F32, name="pw", tag="bank")
            pw4 = pw[:].rearrange("q (a u g) -> q a u g", a=2, u=2)
            wm32 = wm[bk][:].bitcast(F32)
            for a in range(2):
                for u in range(2):
                    o = u * 256 + a * P
                    nc.tensor.transpose(pw4[:, a, u, :], wm32[:, o : o + P], ident[:])
            lo = (bk % 2) * 512
            nc.scalar.copy(
                out=wg[h][:].bitcast(F32)[:, lo : lo + 512].rearrange(
                    "q (a g u) -> q a g u", a=2, u=2
                ),
                in_=pw[:].rearrange("q (a u g) -> q a g u", a=2, u=2),
            )

        def w_quant(h):
            nc.vector.quantize_mx(
                out=w_codes[h][:].bitcast(E4M3X4), scales=w_scales[h][:], in_=wg[h][:]
            )

        g_perm = {}
        g_grp = {}
        g_codes = {}
        g_scales = {}

        def pp(k, on_scalar=False):
            t, off = raw_of_chunk[k]
            gp = perm.tile([P, CH * J], BF16, name="gp")
            dst = gp[:].bitcast(F32).rearrange("q (x e a) -> q x e a", e=32, a=4)
            src = t[:, off : off + CH * J].bitcast(F32).rearrange("q (x a e) -> q x e a", e=32, a=4)
            if on_scalar:
                nc.scalar.copy(out=dst, in_=src)
            else:
                nc.vector.tensor_copy(out=dst, in_=src)
            g_perm[k] = gp

        def tr(k):
            gp32 = g_perm[k][:].bitcast(F32)
            gg = grp.tile([P, CH * J], BF16, name="gg", align_bytes=64)
            g_grp[k] = gg
            for half in range(2):
                pt = psum.tile([P, 512], F32, name="pt", tag="bank")
                pt4 = pt[:].rearrange("q (a u c) -> q a u c", a=2, u=2)
                for a in range(2):
                    for u in range(2):
                        o = ((half * 2 + a) * 2 + u) * P
                        nc.tensor.transpose(pt4[:, a, u, :], gp32[:, o : o + P], ident[:])
                nc.scalar.copy(
                    out=gg[:].bitcast(F32)[:, half * 512 : (half + 1) * 512].rearrange(
                        "q (a c u) -> q a c u", a=2, u=2
                    ),
                    in_=pt[:].rearrange("q (a u c) -> q a c u", a=2, u=2),
                )

        def qz(k):
            cd = keep.tile([P, CH * P], U32, name="g_codes%d" % k, align_bytes=64)
            sc = keep.tile([P, CH * P], U8, name="g_scales%d" % k, align_bytes=64)
            nc.vector.quantize_mx(out=cd[:].bitcast(E5M2X4), scales=sc[:], in_=g_grp[k][:])
            g_codes[k] = cd
            g_scales[k] = sc

        group_of_row = []
        for s in STORE_ROWS:
            first = len(group_of_row)
            for i in range(s):
                group_of_row.append((first, s))
        st_of_group = {}

        def pair(n):
            k = n // CH
            banks = {}
            for h in range(2):
                for r in range(2):
                    nn = n + r - k * CH
                    po = psum.tile([P, 512], F32, name="po", tag="bank")
                    nc.tensor.matmul_mx(
                        out=po[:],
                        lhsT=g_codes[k][:, nn * P : (nn + 1) * P].bitcast(E5M2X4),
                        lhsT_scale=g_scales[k][:, nn * P : (nn + 1) * P],
                        rhs=w_codes[h][:].bitcast(E4M3X4),
                        rhs_scale=w_scales[h][:],
                        start=True,
                        stop=True,
                    )
                    banks[(r, h)] = po
            for r in range(2):
                row = n + r
                first, s = group_of_row[row]
                if row == first:
                    st_of_group[first] = stage[s].tile([P, s * G], F32, name="st%d" % s)
                st = st_of_group[first]
                lo = (row - first) * G
                dst = st[:, lo : lo + G].rearrange("c (q h t) -> c h q t", h=2, t=4)
                for h in range(2):
                    src = banks[(r, h)][:].rearrange("c (t q) -> c q t", t=4)
                    if r == 0:
                        nc.scalar.copy(out=dst[:, h], in_=src)
                    else:
                        nc.vector.tensor_copy(out=dst[:, h], in_=src)
                if row == first + s - 1:
                    nc.sync.dma_start(out=out_d[:, first * G : (first + s) * G], in_=st[:])

        dummy(6)
        pp(0, on_scalar=True)
        w_mul(0, 0)
        w_mul(0, 1)
        w_bank(0)
        dummy(2)
        w_mul(1, 0)
        w_mul(1, 1)
        w_bank(1)
        dummy(1)
        tr(0)
        dummy(2)
        w_mul(2, 0)
        w_mul(2, 1)
        w_bank(2)
        dummy(2)
        w_mul(3, 0)
        w_mul(3, 1)
        w_bank(3)
        dummy(2)
        pp(1)
        w_quant(0)
        qz(0)
        w_quant(1)
        pp(2)
        tr(1)
        for k in range(NCH):
            pair(k * CH)
            if k + 1 < NCH:
                qz(k + 1)
            if k + 2 < NCH:
                tr(k + 2)
            if k + 3 < NCH:
                pp(k + 3)
            pair(k * CH + 2)
